import numpy as np
import ml_dtypes


def mxq(x, axis, fmt="e4m3"):
    dtype, down = {"e4m3": (ml_dtypes.float8_e4m3fn, 7), "e5m2": (ml_dtypes.float8_e5m2, 14)}[fmt]
    v = np.moveaxis(np.asarray(x, np.float32).astype(ml_dtypes.bfloat16).astype(np.float64), axis, -1)
    blocks = v.reshape(v.shape[:-1] + (-1, 32))
    amax = np.abs(blocks).max(-1, keepdims=True)
    byte = np.maximum(np.where(amax > 0, np.frexp(amax)[1] - 1 + 127, 0) - down, 1)
    scale = np.exp2(byte - 127.0)
    codes = (blocks / scale).astype(np.float32).astype(dtype).astype(np.float64)
    return np.moveaxis((codes * scale).reshape(v.shape), -1, axis)


WIDE = False


def mx_kscale(k):
    if not WIDE:
        return np.ones(k)
    levels = np.array([10, -10, 5, -5, 0])
    a = np.random.permutation(np.resize(levels, k // 512 * 4)).reshape(k // 512, 4)
    idx = np.arange(k)
    return np.exp2(a[idx // 512, idx % 128 // 32])


BF16 = ml_dtypes.bfloat16


def bf(x):
    return np.asarray(x, np.float32).astype(BF16)


def f64(x):
    return np.asarray(x).astype(np.float64)


B, NI, NK, NJ, C_Z, C_H = 1, 4096, 512, 256, 128, 4
EPS = 1e-5
KEEP = 0.85


def layer_norm(x, w, b):
    mu = x.mean(-1, keepdims=True)
    var = ((x - mu) ** 2).mean(-1, keepdims=True)
    return (x - mu) / np.sqrt(var + EPS) * w + b


def setup_inputs():
    s = mx_kscale(NK)
    return {"a_gated": bf(np.random.standard_normal((B, NI, NK, C_H)) * 0.55 * s[None, None, :, None]),
            "b_gated": bf(np.random.standard_normal((B, NK, NJ, C_H)) * 0.55 / s[None, :, None, None]),
            "mask_ik": bf(np.random.random((B, NI, NK)) < KEEP),
            "mask_kj": bf(np.random.random((B, NK, NJ)) < KEEP),
            "ln_out_w": bf(1.0 + 0.1 * np.random.standard_normal(C_H)),
            "ln_out_b": bf(0.1 * np.random.standard_normal(C_H))}


def reference(a_gated, b_gated, mask_ik, mask_kj, ln_out_w, ln_out_b):
    a = f64(mask_ik)[..., None] * f64(a_gated)
    b = f64(mask_kj)[..., None] * f64(b_gated)
    at = a.transpose(0, 3, 1, 2)
    bt = b.transpose(0, 3, 1, 2)
    x = (mxq(at, 3, "e4m3") @ mxq(bt, 2, "e4m3")).transpose(0, 2, 3, 1)
    return layer_norm(x, f64(ln_out_w), f64(ln_out_b))

@@ -1,0 +1,213 @@
+from contextlib import ExitStack
+
+import concourse.mybir as mybir
+from concourse.masks import make_identity
+
+BF16 = mybir.dt.bfloat16
+F32 = mybir.dt.float32
+U32 = mybir.dt.uint32
+U8 = mybir.dt.uint8
+FP8X4 = mybir.dt.float8_e4m3fn_x4
+ALU = mybir.AluOpType
+ACT = mybir.ActivationFunctionType
+
+NI, NK, NJ, ND = 4096, 512, 256, 4
+EPS = 1e-5
+FLOPS = 2 * NI * NK * NJ * ND
+
+P = 128
+PACK = 4
+KQ = NK // PACK
+I_BLOCK = P // PACK
+I_TILE = P
+TILES = 2
+ROUND = TILES * I_TILE
+ROUNDS = NI // ROUND
+BLOCKS = ROUND // I_BLOCK
+TILE_BLOCKS = I_TILE // I_BLOCK
+GROUPED = I_TILE * PACK
+
+PAIR_SIGN = (1.0, -1.0, 1.0, -1.0)
+HALF_SIGN = (1.0, 1.0, -1.0, -1.0)
+PLUS, MINUS = 0, 1
+
+
+def tile_trianglemultiplicativeupdate_pa_t_kernel(
+    tc, a_gated, b_gated, mask_ik, mask_kj, ln_out_w, ln_out_b, out
+):
+    nc = tc.nc
+    with ExitStack() as ctx:
+        keep = ctx.enter_context(tc.tile_pool(name="keep", bufs=1))
+        loads = ctx.enter_context(tc.tile_pool(name="loads", bufs=3))
+        front = ctx.enter_context(tc.tile_pool(name="front", bufs=2))
+        norm = ctx.enter_context(tc.tile_pool(name="norm", bufs=2))
+        flipped = ctx.enter_context(tc.psum_pool(name="flipped", bufs=2))
+        sums = ctx.enter_context(tc.psum_pool(name="sums", bufs=2))
+
+        a_rows = a_gated[0].rearrange("i (t q) d -> (i t) (q d)", t=PACK)
+        a_rounds = a_rows.rearrange("(r b p) c -> r p b c", b=BLOCKS, p=P)
+        m_rows = mask_ik[0].rearrange("i (t q) -> (i t) q", t=PACK)
+        m_rounds = m_rows.rearrange("(r b p) c -> r p b c", b=BLOCKS, p=P)
+        out_rounds = out[0].rearrange("(r h p) j d -> r p h (j d)", h=TILES, p=P)
+
+        identity = keep.tile([P, P], BF16)
+        make_identity(nc, identity[:])
+
+        b_raw = keep.tile([P, PACK, NJ * ND], BF16)
+        nc.sync.dma_start(out=b_raw[:], in_=b_gated[0].rearrange("(t q) j d -> q t (j d)", t=PACK))
+        mkj = keep.tile([P, PACK, NJ], BF16)
+        nc.sync.dma_start(out=mkj[:], in_=mask_kj[0].rearrange("(t q) j -> q t j", t=PACK))
+        w_rows = keep.tile([P, ND], BF16)
+        nc.sync.dma_start(out=w_rows[:], in_=ln_out_w.partition_broadcast(P))
+        bias_rows = keep.tile([P, ND], BF16)
+        nc.sync.dma_start(out=bias_rows[:], in_=ln_out_b.partition_broadcast(P))
+
+        b_grouped = keep.tile([P, 2, ND, NJ * PACK], BF16, align_bytes=64)
+        for d in range(ND):
+            nc.vector.tensor_tensor(
+                out=b_grouped[:, PLUS, d, :].rearrange("p (j t) -> p j t", t=PACK),
+                in0=b_raw[:].rearrange("p t (j d) -> p d j t", d=ND)[:, d],
+                in1=mkj[:].rearrange("p t j -> p j t"),
+                op=ALU.mult,
+            )
+        nc.vector.tensor_scalar_mul(
+            out=b_grouped[:, MINUS].rearrange("p d c -> p (d c)"),
+            in0=b_grouped[:, PLUS].rearrange("p d c -> p (d c)"),
+            scalar1=-1.0,
+        )
+        b_codes = keep.tile([P, 2, ND, NJ], U32, align_bytes=64)
+        b_scales = keep.tile([P, 2, ND, NJ], U8, align_bytes=64)
+        for sign in (PLUS, MINUS):
+            nc.vector.quantize_mx(
+                out=b_codes[:, sign].rearrange("p d j -> p (d j)").bitcast(FP8X4),
+                scales=b_scales[:, sign].rearrange("p d j -> p (d j)"),
+                in_=b_grouped[:, sign].rearrange("p d c -> p (d c)"),
+            )
+
+        pair_gain = keep.tile([P, ND], F32)
+        half_gain = keep.tile([P, ND], F32)
+        shift = keep.tile([P, ND], F32)
+        for d in range(ND):
+            nc.vector.tensor_scalar_mul(
+                out=pair_gain[:, d : d + 1], in0=w_rows[:, d : d + 1], scalar1=0.5 * PAIR_SIGN[d]
+            )
+            nc.vector.tensor_scalar_mul(
+                out=half_gain[:, d : d + 1], in0=w_rows[:, d : d + 1], scalar1=HALF_SIGN[d]
+            )
+        nc.vector.tensor_copy(out=shift[:], in_=bias_rows[:])
+
+        def quantise_round(r):
+            a_raw = loads.tile([P, BLOCKS, KQ * ND], BF16)
+            nc.sync.dma_start(out=a_raw[:], in_=a_rounds[r])
+            m_raw = loads.tile([P, BLOCKS, KQ], BF16)
+            nc.sync.dma_start(out=m_raw[:], in_=m_rounds[r])
+
+            m_flip = flipped.tile([P, BLOCKS * P], BF16, tag="flip")
+            for b in range(BLOCKS):
+                nc.tensor.transpose(m_flip[:, b * P : (b + 1) * P], m_raw[:, b, :], identity[:])
+            m_grouped = front.tile([P, TILES, GROUPED], BF16)
+            nc.scalar.copy(out=m_grouped[:].rearrange("p h c -> p (h c)"), in_=m_flip[:])
+
+            a_by_channel = a_raw[:].rearrange("p b (q d) -> p b d q", d=ND)
+            a_grouped = front.tile([P, TILES, ND, GROUPED], BF16, align_bytes=64)
+            a_codes = front.tile([P, TILES, ND, I_TILE], U32, align_bytes=64)
+            a_scales = front.tile([P, TILES, ND, I_TILE], U8, align_bytes=64)
+            for h in range(TILES):
+                for pair in range(ND // 2):
+                    a_flip = flipped.tile([P, 2, GROUPED], BF16, tag="flip")
+                    for e in range(2):
+                        for b in range(TILE_BLOCKS):
+                            nc.tensor.transpose(
+                                a_flip[:, e, b * P : (b + 1) * P],
+                                a_by_channel[:, h * TILE_BLOCKS + b, 2 * pair + e, :],
+                                identity[:],
+                            )
+                    nc.vector.tensor_tensor(
+                        out=a_grouped[:, h, 2 * pair : 2 * pair + 2, :],
+                        in0=a_flip[:],
+                        in1=m_grouped[:, h, :].unsqueeze(1).to_broadcast([P, 2, GROUPED]),
+                        op=ALU.mult,
+                    )
+                nc.vector.quantize_mx(
+                    out=a_codes[:, h].rearrange("p d i -> p (d i)").bitcast(FP8X4),
+                    scales=a_scales[:, h].rearrange("p d i -> p (d i)"),
+                    in_=a_grouped[:, h].rearrange("p d c -> p (d c)"),
+                )
+            return a_codes, a_scales
+
+        def multiply_and_normalise(r, a_codes, a_scales):
+            c1 = sums.tile([P, TILES, NJ], F32)
+            c2 = sums.tile([P, TILES, NJ], F32)
+            c3 = sums.tile([P, TILES, NJ], F32)
+            pair_sums = (c1, c2)
+
+            def mx_pass(acc, h, d, sign, start, stop):
+                nc.tensor.matmul_mx(
+                    out=acc[:, h, :],
+                    lhsT=a_codes[:, h, d, :].bitcast(FP8X4),
+                    lhsT_scale=a_scales[:, h, d, :],
+                    rhs=b_codes[:, sign, d, :].bitcast(FP8X4),
+                    rhs_scale=b_scales[:, sign, d, :],
+                    start=start,
+                    stop=stop,
+                )
+
+            for h in range(TILES):
+                for d in range(ND):
+                    mx_pass(pair_sums[d // 2], h, d, PLUS if PAIR_SIGN[d] > 0 else MINUS,
+                            d % 2 == 0, d % 2 == 1)
+                    mx_pass(c3, h, d, PLUS if HALF_SIGN[d] > 0 else MINUS, d == 0, d == ND - 1)
+
+            wide = TILES * NJ
+            squares = norm.tile([P, 3, wide], F32)
+            for n, c in enumerate((c1, c2, c3)):
+                nc.scalar.square(out=squares[:, n, :], in_=c[:].rearrange("p h j -> p (h j)"))
+            pair_squares = norm.tile([P, wide], F32)
+            nc.vector.tensor_tensor(
+                out=pair_squares[:], in0=squares[:, 0, :], in1=squares[:, 1, :], op=ALU.add
+            )
+            var16 = norm.tile([P, wide], F32)
+            nc.vector.scalar_tensor_tensor(
+                out=var16[:], in0=pair_squares[:], scalar=2.0, in1=squares[:, 2, :],
+                op0=ALU.mult, op1=ALU.add,
+            )
+            rstd = norm.tile([P, wide], F32)
+            nc.scalar.activation(
+                out=rstd[:], in_=var16[:], func=ACT.Abs_reciprocal_sqrt, scale=1.0 / 16.0, bias=EPS
+            )
+            pair_part = norm.tile([P, ND, wide], F32)
+            for d in range(ND):
+                nc.vector.scalar_tensor_tensor(
+                    out=pair_part[:, d, :],
+                    in0=pair_sums[d // 2][:].rearrange("p h j -> p (h j)"),
+                    scalar=pair_gain[:, d : d + 1],
+                    in1=rstd[:],
+                    op0=ALU.mult,
+                    op1=ALU.mult,
+                )
+            half_norm = norm.tile([P, wide], F32)
+            nc.vector.scalar_tensor_tensor(
+                out=half_norm[:], in0=c3[:].rearrange("p h j -> p (h j)"), scalar=0.25,
+                in1=rstd[:], op0=ALU.mult, op1=ALU.mult,
+            )
+            half_part = norm.tile([P, ND, wide], F32)
+            for d in range(ND):
+                nc.scalar.activation(
+                    out=half_part[:, d, :], in_=half_norm[:], func=ACT.Identity,
+                    scale=half_gain[:, d : d + 1], bias=shift[:, d : d + 1],
+                )
+            y = norm.tile([P, TILES, NJ * ND], F32)
+            for h in range(TILES):
+                nc.gpsimd.tensor_tensor(
+                    out=y[:, h, :].rearrange("p (j d) -> p j d", d=ND),
+                    in0=pair_part[:, :, h * NJ : (h + 1) * NJ].rearrange("p d j -> p j d"),
+                    in1=half_part[:, :, h * NJ : (h + 1) * NJ].rearrange("p d j -> p j d"),
+                    op=ALU.add,
+                )
+            nc.sync.dma_start(out=out_rounds[r], in_=y[:])
+
+        ready = quantise_round(0)
+        for r in range(ROUNDS):
+            following = quantise_round(r + 1) if r + 1 < ROUNDS else None
+            multiply_and_normalise(r, ready[0], ready[1])
+            ready = following

@@ -26,6 +26,9 @@ ROUNDS = NI // ROUND
 BLOCKS = ROUND // I_BLOCK
 TILE_BLOCKS = I_TILE // I_BLOCK
 GROUPED = I_TILE * PACK
+PAIRS = ND // 2
+WIDE = TILES * NJ
+AHEAD = 4
 
 PAIR_SIGN = (1.0, -1.0, 1.0, -1.0)
 HALF_SIGN = (1.0, 1.0, -1.0, -1.0)
@@ -37,6 +40,7 @@ def tile_trianglemultiplicativeupdate_pa_t_kernel(
 ):
     nc = tc.nc
     with ExitStack() as ctx:
+        ctx.enter_context(tc.manual_schedule())
         keep = ctx.enter_context(tc.tile_pool(name="keep", bufs=1))
         loads = ctx.enter_context(tc.tile_pool(name="loads", bufs=3))
         front = ctx.enter_context(tc.tile_pool(name="front", bufs=2))
@@ -48,7 +52,160 @@ def tile_trianglemultiplicativeupdate_pa_t_kernel(
         a_rounds = a_rows.rearrange("(r b p) c -> r p b c", b=BLOCKS, p=P)
         m_rows = mask_ik[0].rearrange("i (t q) -> (i t) q", t=PACK)
         m_rounds = m_rows.rearrange("(r b p) c -> r p b c", b=BLOCKS, p=P)
-        out_rounds = out[0].rearrange("(r h p) j d -> r p h (j d)", h=TILES, p=P)
+        out_tiles = out[0].rearrange("(r h p) j d -> r h p (j d)", h=TILES, p=P)
+
+        raw = {}
+        split_tiles = {}
+        mask_tiles = {}
+        operand = {}
+        contrast = {}
+        stats = {}
+
+        def live(r):
+            return 0 <= r < ROUNDS
+
+        def load_round(r):
+            a_raw = loads.tile([P, BLOCKS, KQ * ND], BF16)
+            nc.sync.dma_start(out=a_raw[:], in_=a_rounds[r])
+            m_raw = loads.tile([P, BLOCKS, KQ], BF16)
+            nc.sync.dma_start(out=m_raw[:], in_=m_rounds[r])
+            raw[r] = (a_raw, m_raw)
+
+        def split_channel_pairs(r, h):
+            if h == 0:
+                a_split = front.tile([P, BLOCKS, PAIRS, KQ * 2], BF16, name="a_split")
+                split_tiles[r] = a_split
+            blocks = slice(h * TILE_BLOCKS, (h + 1) * TILE_BLOCKS)
+            nc.scalar.copy(
+                out=split_tiles[r][:, blocks].bitcast(F32),
+                in_=raw[r][0][:, blocks].bitcast(F32).rearrange("p b (q u) -> p b u q", u=PAIRS),
+            )
+
+        def flip_mask(r):
+            m_flip = flipped.tile([P, BLOCKS * P], BF16, tag="flip")
+            for b in range(BLOCKS):
+                nc.tensor.transpose(m_flip[:, b * P : (b + 1) * P], raw[r][1][:, b, :], identity[:])
+            return m_flip
+
+        def keep_mask(r, m_flip):
+            m_grouped = front.tile([P, TILES, GROUPED], BF16)
+            nc.scalar.copy(out=m_grouped[:].rearrange("p h c -> p (h c)"), in_=m_flip[:])
+            mask_tiles[r] = m_grouped
+
+        def flip_and_mask(r, h, pair):
+            if h == 0 and pair == 0:
+                a_grouped = front.tile([P, TILES, ND, GROUPED], BF16, align_bytes=64)
+                a_codes = front.tile([P, TILES, ND, I_TILE], U32, align_bytes=64)
+                a_scales = front.tile([P, TILES, ND, I_TILE], U8, align_bytes=64)
+                operand[r] = (a_grouped, a_codes, a_scales)
+            by_channel = split_tiles[r][:].rearrange("p b u (q e) -> p b u e q", e=2)
+            a_flip = flipped.tile([P, 2, GROUPED], BF16, tag="flip")
+            for e in range(2):
+                for b in range(TILE_BLOCKS):
+                    nc.tensor.transpose(
+                        a_flip[:, e, b * P : (b + 1) * P],
+                        by_channel[:, h * TILE_BLOCKS + b, pair, e, :],
+                        identity[:],
+                    )
+            nc.vector.tensor_tensor(
+                out=operand[r][0][:, h, 2 * pair : 2 * pair + 2, :],
+                in0=a_flip[:],
+                in1=mask_tiles[r][:, h, :].unsqueeze(1).to_broadcast([P, 2, GROUPED]),
+                op=ALU.mult,
+            )
+
+        def quantise(r, h):
+            a_grouped, a_codes, a_scales = operand[r]
+            nc.vector.quantize_mx(
+                out=a_codes[:, h].rearrange("p d i -> p (d i)").bitcast(FP8X4),
+                scales=a_scales[:, h].rearrange("p d i -> p (d i)"),
+                in_=a_grouped[:, h].rearrange("p d c -> p (d c)"),
+            )
+
+        def multiply(r, h, pair):
+            if h == 0 and pair == 0:
+                c1 = sums.tile([P, TILES, NJ], F32)
+                c2 = sums.tile([P, TILES, NJ], F32)
+                c3 = sums.tile([P, TILES, NJ], F32)
+                contrast[r] = (c1, c2, c3)
+            a_codes, a_scales = operand[r][1], operand[r][2]
+            for d in (2 * pair, 2 * pair + 1):
+                for acc, sign, start, stop in (
+                    (contrast[r][pair], PAIR_SIGN[d], d % 2 == 0, d % 2 == 1),
+                    (contrast[r][2], HALF_SIGN[d], d == 0, d == ND - 1),
+                ):
+                    which = PLUS if sign > 0 else MINUS
+                    nc.tensor.matmul_mx(
+                        out=acc[:, h, :],
+                        lhsT=a_codes[:, h, d, :].bitcast(FP8X4),
+                        lhsT_scale=a_scales[:, h, d, :],
+                        rhs=b_codes[:, which, d, :].bitcast(FP8X4),
+                        rhs_scale=b_scales[:, which, d, :],
+                        start=start,
+                        stop=stop,
+                    )
+
+        def flat(c):
+            return c[:].rearrange("p h j -> p (h j)")
+
+        def square_contrast(r, n):
+            if n == 0:
+                squares = norm.tile([P, 3, WIDE], F32)
+                var16 = norm.tile([P, WIDE], F32)
+                rstd = norm.tile([P, WIDE], F32)
+                half_norm = norm.tile([P, WIDE], F32)
+                pair_part = norm.tile([P, ND, WIDE], F32)
+                half_part = norm.tile([P, ND, WIDE], F32)
+                stats[r] = (squares, var16, rstd, half_norm, pair_part, half_part)
+            nc.scalar.square(out=stats[r][0][:, n, :], in_=flat(contrast[r][n]))
+
+        def variance(r):
+            squares, var16 = stats[r][0], stats[r][1]
+            nc.vector.tensor_tensor(
+                out=var16[:], in0=squares[:, 0, :], in1=squares[:, 1, :], op=ALU.add
+            )
+            nc.vector.scalar_tensor_tensor(
+                out=var16[:], in0=var16[:], scalar=2.0, in1=squares[:, 2, :],
+                op0=ALU.mult, op1=ALU.add,
+            )
+
+        def inverse_deviation(r):
+            nc.scalar.activation(
+                out=stats[r][2][:], in_=stats[r][1][:], func=ACT.Abs_reciprocal_sqrt,
+                scale=1.0 / 16.0, bias=EPS,
+            )
+
+        def normalise_half(r):
+            nc.vector.scalar_tensor_tensor(
+                out=stats[r][3][:], in0=flat(contrast[r][2]), scalar=0.25, in1=stats[r][2][:],
+                op0=ALU.mult, op1=ALU.mult,
+            )
+
+        def normalise_pair(r, d):
+            nc.vector.scalar_tensor_tensor(
+                out=stats[r][4][:, d, :], in0=flat(contrast[r][d // 2]),
+                scalar=pair_gain[:, d : d + 1], in1=stats[r][2][:], op0=ALU.mult, op1=ALU.mult,
+            )
+
+        def gain_and_shift(r):
+            for d in range(ND):
+                nc.scalar.activation(
+                    out=stats[r][5][:, d, :], in_=stats[r][3][:], func=ACT.Identity,
+                    scale=half_gain[:, d : d + 1], bias=shift[:, d : d + 1],
+                )
+
+        def combine_and_store(r):
+            pair_part, half_part = stats[r][4], stats[r][5]
+            for h in range(TILES):
+                y = norm.tile([P, NJ * ND], F32, bufs=4)
+                columns = slice(h * NJ, (h + 1) * NJ)
+                nc.gpsimd.tensor_tensor(
+                    out=y[:].rearrange("p (j d) -> p j d", d=ND),
+                    in0=pair_part[:, :, columns].rearrange("p d j -> p j d"),
+                    in1=half_part[:, :, columns].rearrange("p d j -> p j d"),
+                    op=ALU.add,
+                )
+                nc.sync.dma_start(out=out_tiles[r, h], in_=y[:])
 
         identity = keep.tile([P, P], BF16)
         make_identity(nc, identity[:])
@@ -57,10 +214,13 @@ def tile_trianglemultiplicativeupdate_pa_t_kernel(
         nc.sync.dma_start(out=b_raw[:], in_=b_gated[0].rearrange("(t q) j d -> q t (j d)", t=PACK))
         mkj = keep.tile([P, PACK, NJ], BF16)
         nc.sync.dma_start(out=mkj[:], in_=mask_kj[0].rearrange("(t q) j -> q t j", t=PACK))
+        load_round(0)
         w_rows = keep.tile([P, ND], BF16)
         nc.sync.dma_start(out=w_rows[:], in_=ln_out_w.partition_broadcast(P))
         bias_rows = keep.tile([P, ND], BF16)
         nc.sync.dma_start(out=bias_rows[:], in_=ln_out_b.partition_broadcast(P))
+        load_round(1)
+        load_round(2)
 
         b_grouped = keep.tile([P, 2, ND, NJ * PACK], BF16, align_bytes=64)
         for d in range(ND):
@@ -77,11 +237,11 @@ def tile_trianglemultiplicativeupdate_pa_t_kernel(
         )
         b_codes = keep.tile([P, 2, ND, NJ], U32, align_bytes=64)
         b_scales = keep.tile([P, 2, ND, NJ], U8, align_bytes=64)
-        for sign in (PLUS, MINUS):
+        for which in (PLUS, MINUS):
             nc.vector.quantize_mx(
-                out=b_codes[:, sign].rearrange("p d j -> p (d j)").bitcast(FP8X4),
-                scales=b_scales[:, sign].rearrange("p d j -> p (d j)"),
-                in_=b_grouped[:, sign].rearrange("p d c -> p (d c)"),
+                out=b_codes[:, which].rearrange("p d j -> p (d j)").bitcast(FP8X4),
+                scales=b_scales[:, which].rearrange("p d j -> p (d j)"),
+                in_=b_grouped[:, which].rearrange("p d c -> p (d c)"),
             )
 
         pair_gain = keep.tile([P, ND], F32)
@@ -96,118 +256,64 @@ def tile_trianglemultiplicativeupdate_pa_t_kernel(
             )
         nc.vector.tensor_copy(out=shift[:], in_=bias_rows[:])
 
-        def quantise_round(r):
-            a_raw = loads.tile([P, BLOCKS, KQ * ND], BF16)
-            nc.sync.dma_start(out=a_raw[:], in_=a_rounds[r])
-            m_raw = loads.tile([P, BLOCKS, KQ], BF16)
-            nc.sync.dma_start(out=m_raw[:], in_=m_rounds[r])
+        split_channel_pairs(0, 0)
+        split_channel_pairs(0, 1)
+        keep_mask(0, flip_mask(0))
 
-            m_flip = flipped.tile([P, BLOCKS * P], BF16, tag="flip")
-            for b in range(BLOCKS):
-                nc.tensor.transpose(m_flip[:, b * P : (b + 1) * P], m_raw[:, b, :], identity[:])
-            m_grouped = front.tile([P, TILES, GROUPED], BF16)
-            nc.scalar.copy(out=m_grouped[:].rearrange("p h c -> p (h c)"), in_=m_flip[:])
+        for s in range(-1, ROUNDS + 1):
+            done, now, coming, later = s - 1, s, s + 1, s + 2
+            if live(s + AHEAD):
+                load_round(s + AHEAD)
+            if live(later):
+                m_flip = flip_mask(later)
+            if live(done):
+                square_contrast(done, 0)
+            if live(later):
+                keep_mask(later, m_flip)
+            if live(done):
+                square_contrast(done, 1)
+                square_contrast(done, 2)
 
-            a_by_channel = a_raw[:].rearrange("p b (q d) -> p b d q", d=ND)
-            a_grouped = front.tile([P, TILES, ND, GROUPED], BF16, align_bytes=64)
-            a_codes = front.tile([P, TILES, ND, I_TILE], U32, align_bytes=64)
-            a_scales = front.tile([P, TILES, ND, I_TILE], U8, align_bytes=64)
-            for h in range(TILES):
-                for pair in range(ND // 2):
-                    a_flip = flipped.tile([P, 2, GROUPED], BF16, tag="flip")
-                    for e in range(2):
-                        for b in range(TILE_BLOCKS):
-                            nc.tensor.transpose(
-                                a_flip[:, e, b * P : (b + 1) * P],
-                                a_by_channel[:, h * TILE_BLOCKS + b, 2 * pair + e, :],
-                                identity[:],
-                            )
-                    nc.vector.tensor_tensor(
-                        out=a_grouped[:, h, 2 * pair : 2 * pair + 2, :],
-                        in0=a_flip[:],
-                        in1=m_grouped[:, h, :].unsqueeze(1).to_broadcast([P, 2, GROUPED]),
-                        op=ALU.mult,
-                    )
-                nc.vector.quantize_mx(
-                    out=a_codes[:, h].rearrange("p d i -> p (d i)").bitcast(FP8X4),
-                    scales=a_scales[:, h].rearrange("p d i -> p (d i)"),
-                    in_=a_grouped[:, h].rearrange("p d c -> p (d c)"),
-                )
-            return a_codes, a_scales
+            if live(coming):
+                flip_and_mask(coming, 0, 0)
+            if live(now):
+                multiply(now, 0, 0)
+            if live(done):
+                variance(done)
+            if live(later):
+                split_channel_pairs(later, 0)
+            if live(done):
+                inverse_deviation(done)
 
-        def multiply_and_normalise(r, a_codes, a_scales):
-            c1 = sums.tile([P, TILES, NJ], F32)
-            c2 = sums.tile([P, TILES, NJ], F32)
-            c3 = sums.tile([P, TILES, NJ], F32)
-            pair_sums = (c1, c2)
+            if live(coming):
+                flip_and_mask(coming, 0, 1)
+            if live(now):
+                multiply(now, 0, 1)
+            if live(done):
+                normalise_half(done)
+            if live(coming):
+                quantise(coming, 0)
+            if live(later):
+                split_channel_pairs(later, 1)
+            if live(done):
+                gain_and_shift(done)
+                normalise_pair(done, 0)
+                normalise_pair(done, 1)
 
-            def mx_pass(acc, h, d, sign, start, stop):
-                nc.tensor.matmul_mx(
-                    out=acc[:, h, :],
-                    lhsT=a_codes[:, h, d, :].bitcast(FP8X4),
-                    lhsT_scale=a_scales[:, h, d, :],
-                    rhs=b_codes[:, sign, d, :].bitcast(FP8X4),
-                    rhs_scale=b_scales[:, sign, d, :],
-                    start=start,
-                    stop=stop,
-                )
+            if live(coming):
+                flip_and_mask(coming, 1, 0)
+            if live(now):
+                multiply(now, 1, 0)
+            if live(done):
+                normalise_pair(done, 2)
 
-            for h in range(TILES):
-                for d in range(ND):
-                    mx_pass(pair_sums[d // 2], h, d, PLUS if PAIR_SIGN[d] > 0 else MINUS,
-                            d % 2 == 0, d % 2 == 1)
-                    mx_pass(c3, h, d, PLUS if HALF_SIGN[d] > 0 else MINUS, d == 0, d == ND - 1)
-
-            wide = TILES * NJ
-            squares = norm.tile([P, 3, wide], F32)
-            for n, c in enumerate((c1, c2, c3)):
-                nc.scalar.square(out=squares[:, n, :], in_=c[:].rearrange("p h j -> p (h j)"))
-            pair_squares = norm.tile([P, wide], F32)
-            nc.vector.tensor_tensor(
-                out=pair_squares[:], in0=squares[:, 0, :], in1=squares[:, 1, :], op=ALU.add
-            )
-            var16 = norm.tile([P, wide], F32)
-            nc.vector.scalar_tensor_tensor(
-                out=var16[:], in0=pair_squares[:], scalar=2.0, in1=squares[:, 2, :],
-                op0=ALU.mult, op1=ALU.add,
-            )
-            rstd = norm.tile([P, wide], F32)
-            nc.scalar.activation(
-                out=rstd[:], in_=var16[:], func=ACT.Abs_reciprocal_sqrt, scale=1.0 / 16.0, bias=EPS
-            )
-            pair_part = norm.tile([P, ND, wide], F32)
-            for d in range(ND):
-                nc.vector.scalar_tensor_tensor(
-                    out=pair_part[:, d, :],
-                    in0=pair_sums[d // 2][:].rearrange("p h j -> p (h j)"),
-                    scalar=pair_gain[:, d : d + 1],
-                    in1=rstd[:],
-                    op0=ALU.mult,
-                    op1=ALU.mult,
-                )
-            half_norm = norm.tile([P, wide], F32)
-            nc.vector.scalar_tensor_tensor(
-                out=half_norm[:], in0=c3[:].rearrange("p h j -> p (h j)"), scalar=0.25,
-                in1=rstd[:], op0=ALU.mult, op1=ALU.mult,
-            )
-            half_part = norm.tile([P, ND, wide], F32)
-            for d in range(ND):
-                nc.scalar.activation(
-                    out=half_part[:, d, :], in_=half_norm[:], func=ACT.Identity,
-                    scale=half_gain[:, d : d + 1], bias=shift[:, d : d + 1],
-                )
-            y = norm.tile([P, TILES, NJ * ND], F32)
-            for h in range(TILES):
-                nc.gpsimd.tensor_tensor(
-                    out=y[:, h, :].rearrange("p (j d) -> p j d", d=ND),
-                    in0=pair_part[:, :, h * NJ : (h + 1) * NJ].rearrange("p d j -> p j d"),
-                    in1=half_part[:, :, h * NJ : (h + 1) * NJ].rearrange("p d j -> p j d"),
-                    op=ALU.add,
-                )
-            nc.sync.dma_start(out=out_rounds[r], in_=y[:])
-
-        ready = quantise_round(0)
-        for r in range(ROUNDS):
-            following = quantise_round(r + 1) if r + 1 < ROUNDS else None
-            multiply_and_normalise(r, ready[0], ready[1])
-            ready = following
+            if live(coming):
+                flip_and_mask(coming, 1, 1)
+            if live(now):
+                multiply(now, 1, 1)
+            if live(done):
+                normalise_pair(done, 3)
+            if live(coming):
+                quantise(coming, 1)
+            if live(done):
+                combine_and_store(done)

@@ -26,9 +26,6 @@ ROUNDS = NI // ROUND
 BLOCKS = ROUND // I_BLOCK
 TILE_BLOCKS = I_TILE // I_BLOCK
 GROUPED = I_TILE * PACK
-PAIRS = ND // 2
-WIDE = TILES * NJ
-AHEAD = 4
 
 PAIR_SIGN = (1.0, -1.0, 1.0, -1.0)
 HALF_SIGN = (1.0, 1.0, -1.0, -1.0)
@@ -40,7 +37,6 @@ def tile_trianglemultiplicativeupdate_pa_t_kernel(
 ):
     nc = tc.nc
     with ExitStack() as ctx:
-        ctx.enter_context(tc.manual_schedule())
         keep = ctx.enter_context(tc.tile_pool(name="keep", bufs=1))
         loads = ctx.enter_context(tc.tile_pool(name="loads", bufs=3))
         front = ctx.enter_context(tc.tile_pool(name="front", bufs=2))
@@ -52,160 +48,7 @@ def tile_trianglemultiplicativeupdate_pa_t_kernel(
         a_rounds = a_rows.rearrange("(r b p) c -> r p b c", b=BLOCKS, p=P)
         m_rows = mask_ik[0].rearrange("i (t q) -> (i t) q", t=PACK)
         m_rounds = m_rows.rearrange("(r b p) c -> r p b c", b=BLOCKS, p=P)
-        out_tiles = out[0].rearrange("(r h p) j d -> r h p (j d)", h=TILES, p=P)
-
-        raw = {}
-        split_tiles = {}
-        mask_tiles = {}
-        operand = {}
-        contrast = {}
-        stats = {}
-
-        def live(r):
-            return 0 <= r < ROUNDS
-
-        def load_round(r):
-            a_raw = loads.tile([P, BLOCKS, KQ * ND], BF16)
-            nc.sync.dma_start(out=a_raw[:], in_=a_rounds[r])
-            m_raw = loads.tile([P, BLOCKS, KQ], BF16)
-            nc.sync.dma_start(out=m_raw[:], in_=m_rounds[r])
-            raw[r] = (a_raw, m_raw)
-
-        def split_channel_pairs(r, h):
-            if h == 0:
-                a_split = front.tile([P, BLOCKS, PAIRS, KQ * 2], BF16, name="a_split")
-                split_tiles[r] = a_split
-            blocks = slice(h * TILE_BLOCKS, (h + 1) * TILE_BLOCKS)
-            nc.scalar.copy(
-                out=split_tiles[r][:, blocks].bitcast(F32),
-                in_=raw[r][0][:, blocks].bitcast(F32).rearrange("p b (q u) -> p b u q", u=PAIRS),
-            )
-
-        def flip_mask(r):
-            m_flip = flipped.tile([P, BLOCKS * P], BF16, tag="flip")
-            for b in range(BLOCKS):
-                nc.tensor.transpose(m_flip[:, b * P : (b + 1) * P], raw[r][1][:, b, :], identity[:])
-            return m_flip
-
-        def keep_mask(r, m_flip):
-            m_grouped = front.tile([P, TILES, GROUPED], BF16)
-            nc.scalar.copy(out=m_grouped[:].rearrange("p h c -> p (h c)"), in_=m_flip[:])
-            mask_tiles[r] = m_grouped
-
-        def flip_and_mask(r, h, pair):
-            if h == 0 and pair == 0:
-                a_grouped = front.tile([P, TILES, ND, GROUPED], BF16, align_bytes=64)
-                a_codes = front.tile([P, TILES, ND, I_TILE], U32, align_bytes=64)
-                a_scales = front.tile([P, TILES, ND, I_TILE], U8, align_bytes=64)
-                operand[r] = (a_grouped, a_codes, a_scales)
-            by_channel = split_tiles[r][:].rearrange("p b u (q e) -> p b u e q", e=2)
-            a_flip = flipped.tile([P, 2, GROUPED], BF16, tag="flip")
-            for e in range(2):
-                for b in range(TILE_BLOCKS):
-                    nc.tensor.transpose(
-                        a_flip[:, e, b * P : (b + 1) * P],
-                        by_channel[:, h * TILE_BLOCKS + b, pair, e, :],
-                        identity[:],
-                    )
-            nc.vector.tensor_tensor(
-                out=operand[r][0][:, h, 2 * pair : 2 * pair + 2, :],
-                in0=a_flip[:],
-                in1=mask_tiles[r][:, h, :].unsqueeze(1).to_broadcast([P, 2, GROUPED]),
-                op=ALU.mult,
-            )
-
-        def quantise(r, h):
-            a_grouped, a_codes, a_scales = operand[r]
-            nc.vector.quantize_mx(
-                out=a_codes[:, h].rearrange("p d i -> p (d i)").bitcast(FP8X4),
-                scales=a_scales[:, h].rearrange("p d i -> p (d i)"),
-                in_=a_grouped[:, h].rearrange("p d c -> p (d c)"),
-            )
-
-        def multiply(r, h, pair):
-            if h == 0 and pair == 0:
-                c1 = sums.tile([P, TILES, NJ], F32)
-                c2 = sums.tile([P, TILES, NJ], F32)
-                c3 = sums.tile([P, TILES, NJ], F32)
-                contrast[r] = (c1, c2, c3)
-            a_codes, a_scales = operand[r][1], operand[r][2]
-            for d in (2 * pair, 2 * pair + 1):
-                for acc, sign, start, stop in (
-                    (contrast[r][pair], PAIR_SIGN[d], d % 2 == 0, d % 2 == 1),
-                    (contrast[r][2], HALF_SIGN[d], d == 0, d == ND - 1),
-                ):
-                    which = PLUS if sign > 0 else MINUS
-                    nc.tensor.matmul_mx(
-                        out=acc[:, h, :],
-                        lhsT=a_codes[:, h, d, :].bitcast(FP8X4),
-                        lhsT_scale=a_scales[:, h, d, :],
-                        rhs=b_codes[:, which, d, :].bitcast(FP8X4),
-                        rhs_scale=b_scales[:, which, d, :],
-                        start=start,
-                        stop=stop,
-                    )
-
-        def flat(c):
-            return c[:].rearrange("p h j -> p (h j)")
-
-        def square_contrast(r, n):
-            if n == 0:
-                squares = norm.tile([P, 3, WIDE], F32)
-                var16 = norm.tile([P, WIDE], F32)
-                rstd = norm.tile([P, WIDE], F32)
-                half_norm = norm.tile([P, WIDE], F32)
-                pair_part = norm.tile([P, ND, WIDE], F32)
-                half_part = norm.tile([P, ND, WIDE], F32)
-                stats[r] = (squares, var16, rstd, half_norm, pair_part, half_part)
-            nc.scalar.square(out=stats[r][0][:, n, :], in_=flat(contrast[r][n]))
-
-        def variance(r):
-            squares, var16 = stats[r][0], stats[r][1]
-            nc.vector.tensor_tensor(
-                out=var16[:], in0=squares[:, 0, :], in1=squares[:, 1, :], op=ALU.add
-            )
-            nc.vector.scalar_tensor_tensor(
-                out=var16[:], in0=var16[:], scalar=2.0, in1=squares[:, 2, :],
-                op0=ALU.mult, op1=ALU.add,
-            )
-
-        def inverse_deviation(r):
-            nc.scalar.activation(
-                out=stats[r][2][:], in_=stats[r][1][:], func=ACT.Abs_reciprocal_sqrt,
-                scale=1.0 / 16.0, bias=EPS,
-            )
-
-        def normalise_half(r):
-            nc.vector.scalar_tensor_tensor(
-                out=stats[r][3][:], in0=flat(contrast[r][2]), scalar=0.25, in1=stats[r][2][:],
-                op0=ALU.mult, op1=ALU.mult,
-            )
-
-        def normalise_pair(r, d):
-            nc.vector.scalar_tensor_tensor(
-                out=stats[r][4][:, d, :], in0=flat(contrast[r][d // 2]),
-                scalar=pair_gain[:, d : d + 1], in1=stats[r][2][:], op0=ALU.mult, op1=ALU.mult,
-            )
-
-        def gain_and_shift(r):
-            for d in range(ND):
-                nc.scalar.activation(
-                    out=stats[r][5][:, d, :], in_=stats[r][3][:], func=ACT.Identity,
-                    scale=half_gain[:, d : d + 1], bias=shift[:, d : d + 1],
-                )
-
-        def combine_and_store(r):
-            pair_part, half_part = stats[r][4], stats[r][5]
-            for h in range(TILES):
-                y = norm.tile([P, NJ * ND], F32, bufs=4)
-                columns = slice(h * NJ, (h + 1) * NJ)
-                nc.gpsimd.tensor_tensor(
-                    out=y[:].rearrange("p (j d) -> p j d", d=ND),
-                    in0=pair_part[:, :, columns].rearrange("p d j -> p j d"),
-                    in1=half_part[:, :, columns].rearrange("p d j -> p j d"),
-                    op=ALU.add,
-                )
-                nc.sync.dma_start(out=out_tiles[r, h], in_=y[:])
+        out_rounds = out[0].rearrange("(r h p) j d -> r p h (j d)", h=TILES, p=P)
 
         identity = keep.tile([P, P], BF16)
         make_identity(nc, identity[:])
@@ -214,13 +57,10 @@ def tile_trianglemultiplicativeupdate_pa_t_kernel(
         nc.sync.dma_start(out=b_raw[:], in_=b_gated[0].rearrange("(t q) j d -> q t (j d)", t=PACK))
         mkj = keep.tile([P, PACK, NJ], BF16)
         nc.sync.dma_start(out=mkj[:], in_=mask_kj[0].rearrange("(t q) j -> q t j", t=PACK))
-        load_round(0)
         w_rows = keep.tile([P, ND], BF16)
         nc.sync.dma_start(out=w_rows[:], in_=ln_out_w.partition_broadcast(P))
         bias_rows = keep.tile([P, ND], BF16)
         nc.sync.dma_start(out=bias_rows[:], in_=ln_out_b.partition_broadcast(P))
-        load_round(1)
-        load_round(2)
 
         b_grouped = keep.tile([P, 2, ND, NJ * PACK], BF16, align_bytes=64)
         for d in range(ND):
@@ -237,11 +77,11 @@ def tile_trianglemultiplicativeupdate_pa_t_kernel(
         )
         b_codes = keep.tile([P, 2, ND, NJ], U32, align_bytes=64)
         b_scales = keep.tile([P, 2, ND, NJ], U8, align_bytes=64)
-        for which in (PLUS, MINUS):
+        for sign in (PLUS, MINUS):
             nc.vector.quantize_mx(
-                out=b_codes[:, which].rearrange("p d j -> p (d j)").bitcast(FP8X4),
-                scales=b_scales[:, which].rearrange("p d j -> p (d j)"),
-                in_=b_grouped[:, which].rearrange("p d c -> p (d c)"),
+                out=b_codes[:, sign].rearrange("p d j -> p (d j)").bitcast(FP8X4),
+                scales=b_scales[:, sign].rearrange("p d j -> p (d j)"),
+                in_=b_grouped[:, sign].rearrange("p d c -> p (d c)"),
             )
 
         pair_gain = keep.tile([P, ND], F32)
@@ -256,64 +96,118 @@ def tile_trianglemultiplicativeupdate_pa_t_kernel(
             )
         nc.vector.tensor_copy(out=shift[:], in_=bias_rows[:])
 
-        split_channel_pairs(0, 0)
-        split_channel_pairs(0, 1)
-        keep_mask(0, flip_mask(0))
+        def quantise_round(r):
+            a_raw = loads.tile([P, BLOCKS, KQ * ND], BF16)
+            nc.sync.dma_start(out=a_raw[:], in_=a_rounds[r])
+            m_raw = loads.tile([P, BLOCKS, KQ], BF16)
+            nc.sync.dma_start(out=m_raw[:], in_=m_rounds[r])
 
-        for s in range(-1, ROUNDS + 1):
-            done, now, coming, later = s - 1, s, s + 1, s + 2
-            if live(s + AHEAD):
-                load_round(s + AHEAD)
-            if live(later):
-                m_flip = flip_mask(later)
-            if live(done):
-                square_contrast(done, 0)
-            if live(later):
-                keep_mask(later, m_flip)
-            if live(done):
-                square_contrast(done, 1)
-                square_contrast(done, 2)
+            m_flip = flipped.tile([P, BLOCKS * P], BF16, tag="flip")
+            for b in range(BLOCKS):
+                nc.tensor.transpose(m_flip[:, b * P : (b + 1) * P], m_raw[:, b, :], identity[:])
+            m_grouped = front.tile([P, TILES, GROUPED], BF16)
+            nc.scalar.copy(out=m_grouped[:].rearrange("p h c -> p (h c)"), in_=m_flip[:])
 
-            if live(coming):
-                flip_and_mask(coming, 0, 0)
-            if live(now):
-                multiply(now, 0, 0)
-            if live(done):
-                variance(done)
-            if live(later):
-                split_channel_pairs(later, 0)
-            if live(done):
-                inverse_deviation(done)
+            a_by_channel = a_raw[:].rearrange("p b (q d) -> p b d q", d=ND)
+            a_grouped = front.tile([P, TILES, ND, GROUPED], BF16, align_bytes=64)
+            a_codes = front.tile([P, TILES, ND, I_TILE], U32, align_bytes=64)
+            a_scales = front.tile([P, TILES, ND, I_TILE], U8, align_bytes=64)
+            for h in range(TILES):
+                for pair in range(ND // 2):
+                    a_flip = flipped.tile([P, 2, GROUPED], BF16, tag="flip")
+                    for e in range(2):
+                        for b in range(TILE_BLOCKS):
+                            nc.tensor.transpose(
+                                a_flip[:, e, b * P : (b + 1) * P],
+                                a_by_channel[:, h * TILE_BLOCKS + b, 2 * pair + e, :],
+                                identity[:],
+                            )
+                    nc.vector.tensor_tensor(
+                        out=a_grouped[:, h, 2 * pair : 2 * pair + 2, :],
+                        in0=a_flip[:],
+                        in1=m_grouped[:, h, :].unsqueeze(1).to_broadcast([P, 2, GROUPED]),
+                        op=ALU.mult,
+                    )
+                nc.vector.quantize_mx(
+                    out=a_codes[:, h].rearrange("p d i -> p (d i)").bitcast(FP8X4),
+                    scales=a_scales[:, h].rearrange("p d i -> p (d i)"),
+                    in_=a_grouped[:, h].rearrange("p d c -> p (d c)"),
+                )
+            return a_codes, a_scales
 
-            if live(coming):
-                flip_and_mask(coming, 0, 1)
-            if live(now):
-                multiply(now, 0, 1)
-            if live(done):
-                normalise_half(done)
-            if live(coming):
-                quantise(coming, 0)
-            if live(later):
-                split_channel_pairs(later, 1)
-            if live(done):
-                gain_and_shift(done)
-                normalise_pair(done, 0)
-                normalise_pair(done, 1)
+        def multiply_and_normalise(r, a_codes, a_scales):
+            c1 = sums.tile([P, TILES, NJ], F32)
+            c2 = sums.tile([P, TILES, NJ], F32)
+            c3 = sums.tile([P, TILES, NJ], F32)
+            pair_sums = (c1, c2)
 
-            if live(coming):
-                flip_and_mask(coming, 1, 0)
-            if live(now):
-                multiply(now, 1, 0)
-            if live(done):
-                normalise_pair(done, 2)
+            def mx_pass(acc, h, d, sign, start, stop):
+                nc.tensor.matmul_mx(
+                    out=acc[:, h, :],
+                    lhsT=a_codes[:, h, d, :].bitcast(FP8X4),
+                    lhsT_scale=a_scales[:, h, d, :],
+                    rhs=b_codes[:, sign, d, :].bitcast(FP8X4),
+                    rhs_scale=b_scales[:, sign, d, :],
+                    start=start,
+                    stop=stop,
+                )
 
-            if live(coming):
-                flip_and_mask(coming, 1, 1)
-            if live(now):
-                multiply(now, 1, 1)
-            if live(done):
-                normalise_pair(done, 3)
-            if live(coming):
-                quantise(coming, 1)
-            if live(done):
-                combine_and_store(done)
+            for h in range(TILES):
+                for d in range(ND):
+                    mx_pass(pair_sums[d // 2], h, d, PLUS if PAIR_SIGN[d] > 0 else MINUS,
+                            d % 2 == 0, d % 2 == 1)
+                    mx_pass(c3, h, d, PLUS if HALF_SIGN[d] > 0 else MINUS, d == 0, d == ND - 1)
+
+            wide = TILES * NJ
+            squares = norm.tile([P, 3, wide], F32)
+            for n, c in enumerate((c1, c2, c3)):
+                nc.scalar.square(out=squares[:, n, :], in_=c[:].rearrange("p h j -> p (h j)"))
+            pair_squares = norm.tile([P, wide], F32)
+            nc.vector.tensor_tensor(
+                out=pair_squares[:], in0=squares[:, 0, :], in1=squares[:, 1, :], op=ALU.add
+            )
+            var16 = norm.tile([P, wide], F32)
+            nc.vector.scalar_tensor_tensor(
+                out=var16[:], in0=pair_squares[:], scalar=2.0, in1=squares[:, 2, :],
+                op0=ALU.mult, op1=ALU.add,
+            )
+            rstd = norm.tile([P, wide], F32)
+            nc.scalar.activation(
+                out=rstd[:], in_=var16[:], func=ACT.Abs_reciprocal_sqrt, scale=1.0 / 16.0, bias=EPS
+            )
+            pair_part = norm.tile([P, ND, wide], F32)
+            for d in range(ND):
+                nc.vector.scalar_tensor_tensor(
+                    out=pair_part[:, d, :],
+                    in0=pair_sums[d // 2][:].rearrange("p h j -> p (h j)"),
+                    scalar=pair_gain[:, d : d + 1],
+                    in1=rstd[:],
+                    op0=ALU.mult,
+                    op1=ALU.mult,
+                )
+            half_norm = norm.tile([P, wide], F32)
+            nc.vector.scalar_tensor_tensor(
+                out=half_norm[:], in0=c3[:].rearrange("p h j -> p (h j)"), scalar=0.25,
+                in1=rstd[:], op0=ALU.mult, op1=ALU.mult,
+            )
+            half_part = norm.tile([P, ND, wide], F32)
+            for d in range(ND):
+                nc.scalar.activation(
+                    out=half_part[:, d, :], in_=half_norm[:], func=ACT.Identity,
+                    scale=half_gain[:, d : d + 1], bias=shift[:, d : d + 1],
+                )
+            y = norm.tile([P, TILES, NJ * ND], F32)
+            for h in range(TILES):
+                nc.vector.tensor_tensor(
+                    out=y[:, h, :].rearrange("p (j d) -> p j d", d=ND),
+                    in0=pair_part[:, :, h * NJ : (h + 1) * NJ].rearrange("p d j -> p j d"),
+                    in1=half_part[:, :, h * NJ : (h + 1) * NJ].rearrange("p d j -> p j d"),
+                    op=ALU.add,
+                )
+            nc.sync.dma_start(out=out_rounds[r], in_=y[:])
+
+        ready = quantise_round(0)
+        for r in range(ROUNDS):
+            following = quantise_round(r + 1) if r + 1 < ROUNDS else None
+            multiply_and_normalise(r, ready[0], ready[1])
+            ready = following

@@ -198,10 +198,10 @@ def tile_trianglemultiplicativeupdate_pa_t_kernel(
                 )
             y = norm.tile([P, TILES, NJ * ND], F32)
             for h in range(TILES):
-                nc.vector.tensor_tensor(
-                    out=y[:, h, :].rearrange("p (j d) -> p j d", d=ND),
-                    in0=pair_part[:, :, h * NJ : (h + 1) * NJ].rearrange("p d j -> p j d"),
-                    in1=half_part[:, :, h * NJ : (h + 1) * NJ].rearrange("p d j -> p j d"),
+                nc.gpsimd.tensor_tensor(
+                    out=y[:, h, :].rearrange("p (g n d) -> p g d n", n=2, d=ND),
+                    in0=pair_part[:, :, h * NJ : (h + 1) * NJ].rearrange("p d (g n) -> p g d n", n=2),
+                    in1=half_part[:, :, h * NJ : (h + 1) * NJ].rearrange("p d (g n) -> p g d n", n=2),
                     op=ALU.add,
                 )
             nc.sync.dma_start(out=out_rounds[r], in_=y[:])

@@ -48,10 +48,19 @@ def tile_trianglemultiplicativeupdate_pa_t_kernel(
         a_rounds = a_rows.rearrange("(r b p) c -> r p b c", b=BLOCKS, p=P)
         m_rows = mask_ik[0].rearrange("i (t q) -> (i t) q", t=PACK)
         m_rounds = m_rows.rearrange("(r b p) c -> r p b c", b=BLOCKS, p=P)
-        out_rounds = out[0].rearrange("(r h p) j d -> r p h (j d)", h=TILES, p=P)
+        out_tiles = out[0].rearrange("(r h p) j d -> r h p (j d)", h=TILES, p=P)
 
         identity = keep.tile([P, P], BF16)
         make_identity(nc, identity[:])
+
+        def load_round(r):
+            a_raw = loads.tile([P, BLOCKS, KQ * ND], BF16)
+            nc.sync.dma_start(out=a_raw[:], in_=a_rounds[r])
+            m_raw = loads.tile([P, BLOCKS, KQ], BF16)
+            nc.sync.dma_start(out=m_raw[:], in_=m_rounds[r])
+            return a_raw, m_raw
+
+        first_raw = load_round(0)
 
         b_raw = keep.tile([P, PACK, NJ * ND], BF16)
         nc.sync.dma_start(out=b_raw[:], in_=b_gated[0].rearrange("(t q) j d -> q t (j d)", t=PACK))
@@ -89,7 +98,7 @@ def tile_trianglemultiplicativeupdate_pa_t_kernel(
         shift = keep.tile([P, ND], F32)
         for d in range(ND):
             nc.vector.tensor_scalar_mul(
-                out=pair_gain[:, d : d + 1], in0=w_rows[:, d : d + 1], scalar1=0.5 * PAIR_SIGN[d]
+                out=pair_gain[:, d : d + 1], in0=w_rows[:, d : d + 1], scalar1=PAIR_SIGN[d]
             )
             nc.vector.tensor_scalar_mul(
                 out=half_gain[:, d : d + 1], in0=w_rows[:, d : d + 1], scalar1=HALF_SIGN[d]
@@ -97,10 +106,7 @@ def tile_trianglemultiplicativeupdate_pa_t_kernel(
         nc.vector.tensor_copy(out=shift[:], in_=bias_rows[:])
 
         def quantise_round(r):
-            a_raw = loads.tile([P, BLOCKS, KQ * ND], BF16)
-            nc.sync.dma_start(out=a_raw[:], in_=a_rounds[r])
-            m_raw = loads.tile([P, BLOCKS, KQ], BF16)
-            nc.sync.dma_start(out=m_raw[:], in_=m_rounds[r])
+            a_raw, m_raw = load_round(r) if r > 0 else first_raw
 
             m_flip = flipped.tile([P, BLOCKS * P], BF16, tag="flip")
             for b in range(BLOCKS):
@@ -175,15 +181,21 @@ def tile_trianglemultiplicativeupdate_pa_t_kernel(
             nc.scalar.activation(
                 out=rstd[:], in_=var16[:], func=ACT.Abs_reciprocal_sqrt, scale=1.0 / 16.0, bias=EPS
             )
-            pair_part = norm.tile([P, ND, wide], F32)
-            for d in range(ND):
+            pair_norm = norm.tile([P, 2, wide], F32)
+            for n in range(2):
                 nc.vector.scalar_tensor_tensor(
-                    out=pair_part[:, d, :],
-                    in0=pair_sums[d // 2][:].rearrange("p h j -> p (h j)"),
-                    scalar=pair_gain[:, d : d + 1],
+                    out=pair_norm[:, n, :],
+                    in0=pair_sums[n][:].rearrange("p h j -> p (h j)"),
+                    scalar=0.5,
                     in1=rstd[:],
                     op0=ALU.mult,
                     op1=ALU.mult,
+                )
+            pair_part = norm.tile([P, ND, wide], F32)
+            for d in range(ND):
+                nc.scalar.activation(
+                    out=pair_part[:, d, :], in_=pair_norm[:, d // 2, :], func=ACT.Identity,
+                    scale=pair_gain[:, d : d + 1],
                 )
             half_norm = norm.tile([P, wide], F32)
             nc.vector.scalar_tensor_tensor(
@@ -197,14 +209,14 @@ def tile_trianglemultiplicativeupdate_pa_t_kernel(
                     scale=half_gain[:, d : d + 1], bias=shift[:, d : d + 1],
                 )
             y = norm.tile([P, TILES, NJ * ND], F32)
-            for h in range(TILES):
-                nc.gpsimd.tensor_tensor(
+            for h, engine in enumerate((nc.gpsimd, nc.vector)):
+                engine.tensor_tensor(
                     out=y[:, h, :].rearrange("p (g n d) -> p g d n", n=2, d=ND),
                     in0=pair_part[:, :, h * NJ : (h + 1) * NJ].rearrange("p d (g n) -> p g d n", n=2),
                     in1=half_part[:, :, h * NJ : (h + 1) * NJ].rearrange("p d (g n) -> p g d n", n=2),
                     op=ALU.add,
                 )
-            nc.sync.dma_start(out=out_rounds[r], in_=y[:])
+                nc.sync.dma_start(out=out_tiles[r, h], in_=y[:, h, :])
 
         ready = quantise_round(0)
         for r in range(ROUNDS):

@@ -209,8 +209,8 @@ def tile_trianglemultiplicativeupdate_pa_t_kernel(
                     scale=half_gain[:, d : d + 1], bias=shift[:, d : d + 1],
                 )
             y = norm.tile([P, TILES, NJ * ND], F32)
-            for h, engine in enumerate((nc.gpsimd, nc.vector)):
-                engine.tensor_tensor(
+            for h in range(TILES):
+                nc.gpsimd.tensor_tensor(
                     out=y[:, h, :].rearrange("p (g n d) -> p g d n", n=2, d=ND),
                     in0=pair_part[:, :, h * NJ : (h + 1) * NJ].rearrange("p d (g n) -> p g d n", n=2),
                     in1=half_part[:, :, h * NJ : (h + 1) * NJ].rearrange("p d (g n) -> p g d n", n=2),

from contextlib import ExitStack

import concourse.mybir as mybir
from concourse.masks import make_identity

BF16 = mybir.dt.bfloat16
F32 = mybir.dt.float32
U32 = mybir.dt.uint32
U8 = mybir.dt.uint8
FP8X4 = mybir.dt.float8_e4m3fn_x4
ALU = mybir.AluOpType
ACT = mybir.ActivationFunctionType

NI, NK, NJ, ND = 4096, 512, 256, 4
EPS = 1e-5
FLOPS = 2 * NI * NK * NJ * ND

P = 128
PACK = 4
KQ = NK // PACK
I_BLOCK = P // PACK
I_TILE = P
TILES = 2
ROUND = TILES * I_TILE
ROUNDS = NI // ROUND
BLOCKS = ROUND // I_BLOCK
TILE_BLOCKS = I_TILE // I_BLOCK
GROUPED = I_TILE * PACK

PAIR_SIGN = (1.0, -1.0, 1.0, -1.0)
HALF_SIGN = (1.0, 1.0, -1.0, -1.0)
PLUS, MINUS = 0, 1


def tile_trianglemultiplicativeupdate_pa_t_kernel(
    tc, a_gated, b_gated, mask_ik, mask_kj, ln_out_w, ln_out_b, out
):
    nc = tc.nc
    with ExitStack() as ctx:
        keep = ctx.enter_context(tc.tile_pool(name="keep", bufs=1))
        loads = ctx.enter_context(tc.tile_pool(name="loads", bufs=3))
        front = ctx.enter_context(tc.tile_pool(name="front", bufs=2))
        norm = ctx.enter_context(tc.tile_pool(name="norm", bufs=2))
        flipped = ctx.enter_context(tc.psum_pool(name="flipped", bufs=2))
        sums = ctx.enter_context(tc.psum_pool(name="sums", bufs=2))

        a_rows = a_gated[0].rearrange("i (t q) d -> (i t) (q d)", t=PACK)
        a_rounds = a_rows.rearrange("(r b p) c -> r p b c", b=BLOCKS, p=P)
        m_rows = mask_ik[0].rearrange("i (t q) -> (i t) q", t=PACK)
        m_rounds = m_rows.rearrange("(r b p) c -> r p b c", b=BLOCKS, p=P)
        out_tiles = out[0].rearrange("(r h p) j d -> r h p (j d)", h=TILES, p=P)

        identity = keep.tile([P, P], BF16)
        make_identity(nc, identity[:])

        def load_round(r):
            a_raw = loads.tile([P, BLOCKS, KQ * ND], BF16)
            nc.sync.dma_start(out=a_raw[:], in_=a_rounds[r])
            m_raw = loads.tile([P, BLOCKS, KQ], BF16)
            nc.sync.dma_start(out=m_raw[:], in_=m_rounds[r])
            return a_raw, m_raw

        first_raw = load_round(0)

        b_raw = keep.tile([P, PACK, NJ * ND], BF16)
        nc.sync.dma_start(out=b_raw[:], in_=b_gated[0].rearrange("(t q) j d -> q t (j d)", t=PACK))
        mkj = keep.tile([P, PACK, NJ], BF16)
        nc.sync.dma_start(out=mkj[:], in_=mask_kj[0].rearrange("(t q) j -> q t j", t=PACK))
        w_rows = keep.tile([P, ND], BF16)
        nc.sync.dma_start(out=w_rows[:], in_=ln_out_w.partition_broadcast(P))
        bias_rows = keep.tile([P, ND], BF16)
        nc.sync.dma_start(out=bias_rows[:], in_=ln_out_b.partition_broadcast(P))

        b_grouped = keep.tile([P, 2, ND, NJ * PACK], BF16, align_bytes=64)
        for d in range(ND):
            nc.vector.tensor_tensor(
                out=b_grouped[:, PLUS, d, :].rearrange("p (j t) -> p j t", t=PACK),
                in0=b_raw[:].rearrange("p t (j d) -> p d j t", d=ND)[:, d],
                in1=mkj[:].rearrange("p t j -> p j t"),
                op=ALU.mult,
            )
        nc.vector.tensor_scalar_mul(
            out=b_grouped[:, MINUS].rearrange("p d c -> p (d c)"),
            in0=b_grouped[:, PLUS].rearrange("p d c -> p (d c)"),
            scalar1=-1.0,
        )
        b_codes = keep.tile([P, 2, ND, NJ], U32, align_bytes=64)
        b_scales = keep.tile([P, 2, ND, NJ], U8, align_bytes=64)
        for sign in (PLUS, MINUS):
            nc.vector.quantize_mx(
                out=b_codes[:, sign].rearrange("p d j -> p (d j)").bitcast(FP8X4),
                scales=b_scales[:, sign].rearrange("p d j -> p (d j)"),
                in_=b_grouped[:, sign].rearrange("p d c -> p (d c)"),
            )

        pair_gain = keep.tile([P, ND], F32)
        half_gain = keep.tile([P, ND], F32)
        shift = keep.tile([P, ND], F32)
        for d in range(ND):
            nc.vector.tensor_scalar_mul(
                out=pair_gain[:, d : d + 1], in0=w_rows[:, d : d + 1], scalar1=PAIR_SIGN[d]
            )
            nc.vector.tensor_scalar_mul(
                out=half_gain[:, d : d + 1], in0=w_rows[:, d : d + 1], scalar1=HALF_SIGN[d]
            )
        nc.vector.tensor_copy(out=shift[:], in_=bias_rows[:])

        def quantise_round(r):
            a_raw, m_raw = load_round(r) if r > 0 else first_raw

            m_flip = flipped.tile([P, BLOCKS * P], BF16, tag="flip")
            for b in range(BLOCKS):
                nc.tensor.transpose(m_flip[:, b * P : (b + 1) * P], m_raw[:, b, :], identity[:])
            m_grouped = front.tile([P, TILES, GROUPED], BF16)
            nc.scalar.copy(out=m_grouped[:].rearrange("p h c -> p (h c)"), in_=m_flip[:])

            a_by_channel = a_raw[:].rearrange("p b (q d) -> p b d q", d=ND)
            a_grouped = front.tile([P, TILES, ND, GROUPED], BF16, align_bytes=64)
            a_codes = front.tile([P, TILES, ND, I_TILE], U32, align_bytes=64)
            a_scales = front.tile([P, TILES, ND, I_TILE], U8, align_bytes=64)
            for h in range(TILES):
                for pair in range(ND // 2):
                    a_flip = flipped.tile([P, 2, GROUPED], BF16, tag="flip")
                    for e in range(2):
                        for b in range(TILE_BLOCKS):
                            nc.tensor.transpose(
                                a_flip[:, e, b * P : (b + 1) * P],
                                a_by_channel[:, h * TILE_BLOCKS + b, 2 * pair + e, :],
                                identity[:],
                            )
                    nc.vector.tensor_tensor(
                        out=a_grouped[:, h, 2 * pair : 2 * pair + 2, :],
                        in0=a_flip[:],
                        in1=m_grouped[:, h, :].unsqueeze(1).to_broadcast([P, 2, GROUPED]),
                        op=ALU.mult,
                    )
                nc.vector.quantize_mx(
                    out=a_codes[:, h].rearrange("p d i -> p (d i)").bitcast(FP8X4),
                    scales=a_scales[:, h].rearrange("p d i -> p (d i)"),
                    in_=a_grouped[:, h].rearrange("p d c -> p (d c)"),
                )
            return a_codes, a_scales

        def multiply_and_normalise(r, a_codes, a_scales):
            c1 = sums.tile([P, TILES, NJ], F32)
            c2 = sums.tile([P, TILES, NJ], F32)
            c3 = sums.tile([P, TILES, NJ], F32)
            pair_sums = (c1, c2)

            def mx_pass(acc, h, d, sign, start, stop):
                nc.tensor.matmul_mx(
                    out=acc[:, h, :],
                    lhsT=a_codes[:, h, d, :].bitcast(FP8X4),
                    lhsT_scale=a_scales[:, h, d, :],
                    rhs=b_codes[:, sign, d, :].bitcast(FP8X4),
                    rhs_scale=b_scales[:, sign, d, :],
                    start=start,
                    stop=stop,
                )

            for h in range(TILES):
                for d in range(ND):
                    mx_pass(pair_sums[d // 2], h, d, PLUS if PAIR_SIGN[d] > 0 else MINUS,
                            d % 2 == 0, d % 2 == 1)
                    mx_pass(c3, h, d, PLUS if HALF_SIGN[d] > 0 else MINUS, d == 0, d == ND - 1)

            wide = TILES * NJ
            squares = norm.tile([P, 3, wide], F32)
            for n, c in enumerate((c1, c2, c3)):
                nc.scalar.square(out=squares[:, n, :], in_=c[:].rearrange("p h j -> p (h j)"))
            pair_squares = norm.tile([P, wide], F32)
            nc.vector.tensor_tensor(
                out=pair_squares[:], in0=squares[:, 0, :], in1=squares[:, 1, :], op=ALU.add
            )
            var16 = norm.tile([P, wide], F32)
            nc.vector.scalar_tensor_tensor(
                out=var16[:], in0=pair_squares[:], scalar=2.0, in1=squares[:, 2, :],
                op0=ALU.mult, op1=ALU.add,
            )
            rstd = norm.tile([P, wide], F32)
            nc.scalar.activation(
                out=rstd[:], in_=var16[:], func=ACT.Abs_reciprocal_sqrt, scale=1.0 / 16.0, bias=EPS
            )
            pair_norm = norm.tile([P, 2, wide], F32)
            for n in range(2):
                nc.vector.scalar_tensor_tensor(
                    out=pair_norm[:, n, :],
                    in0=pair_sums[n][:].rearrange("p h j -> p (h j)"),
                    scalar=0.5,
                    in1=rstd[:],
                    op0=ALU.mult,
                    op1=ALU.mult,
                )
            pair_part = norm.tile([P, ND, wide], F32)
            for d in range(ND):
                nc.scalar.activation(
                    out=pair_part[:, d, :], in_=pair_norm[:, d // 2, :], func=ACT.Identity,
                    scale=pair_gain[:, d : d + 1],
                )
            half_norm = norm.tile([P, wide], F32)
            nc.vector.scalar_tensor_tensor(
                out=half_norm[:], in0=c3[:].rearrange("p h j -> p (h j)"), scalar=0.25,
                in1=rstd[:], op0=ALU.mult, op1=ALU.mult,
            )
            half_part = norm.tile([P, ND, wide], F32)
            for d in range(ND):
                nc.scalar.activation(
                    out=half_part[:, d, :], in_=half_norm[:], func=ACT.Identity,
                    scale=half_gain[:, d : d + 1], bias=shift[:, d : d + 1],
                )
            y = norm.tile([P, TILES, NJ * ND], F32)
            for h in range(TILES):
                nc.gpsimd.tensor_tensor(
                    out=y[:, h, :].rearrange("p (g n d) -> p g d n", n=2, d=ND),
                    in0=pair_part[:, :, h * NJ : (h + 1) * NJ].rearrange("p d (g n) -> p g d n", n=2),
                    in1=half_part[:, :, h * NJ : (h + 1) * NJ].rearrange("p d (g n) -> p g d n", n=2),
                    op=ALU.add,
                )
                nc.sync.dma_start(out=out_tiles[r, h], in_=y[:, h, :])

        ready = quantise_round(0)
        for r in range(ROUNDS):
            following = quantise_round(r + 1) if r + 1 < ROUNDS else None
            multiply_and_normalise(r, ready[0], ready[1])
            ready = following
